import numpy as np
import ml_dtypes


def mxq(x, axis, fmt="e4m3"):
    dtype, down = {"e4m3": (ml_dtypes.float8_e4m3fn, 7), "e5m2": (ml_dtypes.float8_e5m2, 14)}[fmt]
    v = np.moveaxis(np.asarray(x, np.float32).astype(ml_dtypes.bfloat16).astype(np.float64), axis, -1)
    blocks = v.reshape(v.shape[:-1] + (-1, 32))
    amax = np.abs(blocks).max(-1, keepdims=True)
    byte = np.maximum(np.where(amax > 0, np.frexp(amax)[1] - 1 + 127, 0) - down, 1)
    scale = np.exp2(byte - 127.0)
    codes = (blocks / scale).astype(np.float32).astype(dtype).astype(np.float64)
    return np.moveaxis((codes * scale).reshape(v.shape), -1, axis)


WIDE = False


def mx_kscale(k):
    if not WIDE:
        return np.ones(k)
    levels = np.array([10, -10, 5, -5, 0])
    a = np.random.permutation(np.resize(levels, k // 512 * 4)).reshape(k // 512, 4)
    idx = np.arange(k)
    return np.exp2(a[idx // 512, idx % 128 // 32])


BF16 = ml_dtypes.bfloat16


def bf(x):
    return np.asarray(x, np.float32).astype(BF16)


def f64(x):
    return np.asarray(x).astype(np.float64)


B, L1, L2, D = 4, 1024, 512, 512
NEG = -1e30


def setup_inputs():
    s = mx_kscale(D)
    return {"q": bf(np.random.standard_normal((B, L1, D)) * 1.4),
            "k": bf(np.random.standard_normal((B, L2, D)) * 1.4),
            "x1": bf(np.random.standard_normal((B, L1, D)) * s),
            "x2": bf(np.random.standard_normal((B, L2, D)) * s),
            "mask": bf(np.random.uniform(size=(B, L2)) > 0.1),
            "Wv": bf(np.random.standard_normal((D, D)) * 1.5 / np.sqrt(D) / s[None, :]),
            "bv": bf(np.random.standard_normal(D) * 0.5)}


def reference(q, k, x1, x2, mask, Wv, bv):
    m = f64(mask)
    wvq = mxq(f64(Wv), 1, "e4m3")
    v2 = (mxq(f64(x2), 2, "e4m3") @ wvq.T) + f64(bv)
    v1 = (mxq(f64(x1), 2, "e4m3") @ wvq.T) + f64(bv)
    a = f64(q) @ f64(k).transpose(0, 2, 1) * (1.0 / np.sqrt(D))
    a = a + (1.0 - m)[:, None, :] * NEG
    e2 = np.exp(a - a.max(2, keepdims=True))
    x2_out = (mxq(e2, 2, "e4m3") @ mxq(v2, 1, "e4m3")) / e2.sum(2, keepdims=True)
    e1 = np.exp(a - a.max(1, keepdims=True))
    x1_mid = (mxq(e1, 1, "e4m3").transpose(0, 2, 1) @ mxq(v1, 1, "e4m3")) / e1.sum(1)[:, :, None]
    x1_mid = x1_mid * m[:, :, None]
    return x2_out, x1_mid

@@ -1,0 +1,431 @@
+import math
+from contextlib import ExitStack
+
+import concourse.mybir as mybir
+from concourse.masks import make_identity
+
+F32 = mybir.dt.float32
+BF16 = mybir.dt.bfloat16
+U32 = mybir.dt.uint32
+U8 = mybir.dt.uint8
+FP8X4 = mybir.dt.float8_e4m3fn_x4
+ALU = mybir.AluOpType
+ACT = mybir.ActivationFunctionType
+AXIS = mybir.AxisListType
+
+B, L1, L2, D = 4, 1024, 512, 512
+P = 128
+PACK = 4
+BANK = 512
+FLOPS = 2 * B * (L1 * D * D + L2 * D * D + 3 * L1 * L2 * D)
+
+SCALE = 1.0 / math.sqrt(D)
+MASKED = 2.0**104
+
+QUARTERS = 4
+UNITS = QUARTERS * B
+AT_INPUTS = 0
+AT_SCORES = 2
+AT_E1 = 3
+AT_PROJECT = 4
+AT_ROWS = 5
+AT_E2 = 6
+AT_OUTPUTS = 8
+STEPS = UNITS + AT_OUTPUTS
+LOAD_AHEAD = 8
+
+
+def tile_coattention_pa_t_kernel(tc, q, k, x1, x2, mask, Wv, bv, out_0, out_1):
+    nc = tc.nc
+    with ExitStack() as ctx:
+        const = ctx.enter_context(tc.tile_pool(name="const", bufs=1))
+        inputs = ctx.enter_context(tc.tile_pool(name="inputs", bufs=4))
+        turned = ctx.enter_context(tc.tile_pool(name="turned", bufs=2))
+        grouped = ctx.enter_context(tc.tile_pool(name="grouped", bufs=2))
+        packed = ctx.enter_context(tc.tile_pool(name="packed", bufs=2))
+        scores = ctx.enter_context(tc.tile_pool(name="scores", bufs=8))
+        exps = ctx.enter_context(tc.tile_pool(name="exps", bufs=3))
+        results = ctx.enter_context(tc.tile_pool(name="results", bufs=3))
+        psum = ctx.enter_context(tc.psum_pool(name="psum", bufs=8))
+        ctx.enter_context(tc.manual_schedule())
+
+        def transpose_words(words):
+            bank = psum.tile([P, 2, 2, P], F32, tag="bank")
+            for block in range(2):
+                for u in range(2):
+                    nc.tensor.transpose(
+                        bank[:, block, u, :], words[:, block, u * P : (u + 1) * P], ident[:]
+                    )
+            return bank
+
+        def group_words(bank, group):
+            nc.scalar.copy(
+                out=group.bitcast(F32).rearrange("p (c r u) -> p c r u", c=2, u=2),
+                in_=bank[:].rearrange("p c u r -> p c r u"),
+            )
+
+        def unit_of(step, offset):
+            n = step - offset
+            return divmod(n, QUARTERS) if 0 <= n < UNITS else None
+
+        ident = const.tile([P, P], F32)
+        make_identity(nc, ident[:])
+
+        col_max = const.tile([P, 2 * UNITS], F32)
+        col_shift = const.tile([P, UNITS], F32)
+        col_sum = const.tile([P, UNITS], F32)
+        col_weight = const.tile([P, UNITS], F32)
+        row_max = const.tile([P, 2 * UNITS], F32)
+        row_shift = const.tile([P, 2 * UNITS], F32)
+        row_sum = const.tile([P, 2 * UNITS], F32)
+        row_weight = const.tile([P, 2 * UNITS], F32)
+
+        loaded = {}
+
+        def load(n):
+            b, quarter = divmod(n, QUARTERS)
+            half = quarter % 2
+            if quarter < 2:
+                q_half = inputs.tile([P, 4, D], BF16)
+                rows = q[b, half * 512 : (half + 1) * 512, :]
+                nc.sync.dma_start(out=q_half[:], in_=rows.rearrange("(c m) d -> m c d", m=P))
+                k_half = inputs.tile([P, 2, D], BF16)
+                rows = k[b, half * 256 : (half + 1) * 256, :]
+                nc.sync.dma_start(out=k_half[:], in_=rows.rearrange("(c m) d -> m c d", m=P))
+                loaded[n] = (q_half, k_half)
+            else:
+                x1_half = inputs.tile([P, 2, 2, D], BF16)
+                rows = x1[b, half * 512 : (half + 1) * 512, :]
+                nc.sync.dma_start(
+                    out=x1_half[:], in_=rows.rearrange("(u m e) d -> m u e d", u=2, e=2)
+                )
+                x2_half = inputs.tile([P, 2, D], BF16)
+                rows = x2[b, half * 256 : (half + 1) * 256, :]
+                nc.sync.dma_start(out=x2_half[:], in_=rows.rearrange("(m e) d -> m e d", e=2))
+                loaded[n] = (x1_half, x2_half)
+
+        wv_rows = const.tile([P, 4, D], BF16)
+        nc.scalar.dma_start(out=wv_rows[:], in_=Wv.rearrange("(c m) d -> m c d", m=P))
+        mask_rows = const.tile([P, P], BF16)
+        nc.vector.memset(mask_rows[:], 0.0)
+        nc.scalar.dma_start(
+            out=mask_rows[0:UNITS, :], in_=mask.rearrange("b (j p) -> (b j) p", p=P)
+        )
+        for n in range(4):
+            load(n)
+        bias = const.tile([P, D], BF16)
+        nc.sync.dma_start(out=bias[:], in_=bv.partition_broadcast(P))
+        for n in range(4, LOAD_AHEAD):
+            load(n)
+
+        mask_f32 = const.tile([P, P], F32)
+        nc.vector.tensor_copy(out=mask_f32[:], in_=mask_rows[:])
+        mask_bank = psum.tile([P, P], F32, tag="bank")
+        nc.tensor.transpose(mask_bank[:], mask_f32[:], ident[:])
+        keep = const.tile([P, UNITS], F32)
+        nc.vector.tensor_copy(out=keep[:], in_=mask_bank[:, 0:UNITS])
+        mask_term = const.tile([P, UNITS], F32)
+        nc.vector.tensor_scalar(
+            out=mask_term[:], in0=keep[:], scalar1=-1.0, scalar2=MASKED, op0=ALU.add, op1=ALU.mult
+        )
+
+        wv_group = const.tile([P, D * PACK], BF16, align_bytes=64)
+        wv_codes = const.tile([P, D], U32, align_bytes=64)
+        wv_scales = const.tile([P, D], U8, align_bytes=64)
+        wv_words = wv_rows[:].bitcast(F32)
+        for pair in range(2):
+            bank = transpose_words(wv_words[:, 2 * pair : 2 * pair + 2, :])
+            group_words(bank, wv_group[:, pair * 1024 : (pair + 1) * 1024])
+        nc.vector.quantize_mx(
+            out=wv_codes[:].bitcast(FP8X4), scales=wv_scales[:], in_=wv_group[:]
+        )
+
+        q_turned, k_turned = {}, {}
+        x_codes, x_scales = {}, {}
+        v_codes, v_scales = {}, {}
+        a_turned = {}
+        e1_codes, e1_scales = {}, {}
+        e2_rows = {}
+        e2_codes, e2_scales = {}, {}
+
+        def transpose_q_k(b, half):
+            q_half, k_half = loaded[QUARTERS * b + half]
+            if half == 0:
+                q_words = turned.tile([P, 2, L1], F32)
+                k_words = turned.tile([P, 2, L2], F32)
+                q_turned[b] = q_words
+                k_turned[b] = k_words
+            words = q_half[:].bitcast(F32)
+            for pair in range(2):
+                bank = transpose_words(words[:, 2 * pair : 2 * pair + 2, :])
+                first = half * 512 + pair * 256
+                nc.scalar.copy(
+                    out=q_turned[b][:, :, first : first + 256].rearrange(
+                        "p u (c r) -> p u c r", c=2
+                    ),
+                    in_=bank[:].rearrange("p c u r -> p u c r"),
+                )
+            bank = transpose_words(k_half[:].bitcast(F32))
+            first = half * 256
+            nc.scalar.copy(
+                out=k_turned[b][:, :, first : first + 256].rearrange("p u (c r) -> p u c r", c=2),
+                in_=bank[:].rearrange("p c u r -> p u c r"),
+            )
+
+        def transpose_x(b, half):
+            x1_half, x2_half = loaded[QUARTERS * b + 2 + half]
+            if half == 0:
+                codes = packed.tile([P, 12 * P], U32, tag="x_codes", align_bytes=64)
+                scales = packed.tile([P, 12 * P], U8, tag="x_scales", align_bytes=64)
+                x_codes[b] = codes
+                x_scales[b] = scales
+            x1_group = grouped.tile([P, 4 * P * PACK], BF16, align_bytes=64)
+            words = x1_half[:].bitcast(F32)
+            for u in range(2):
+                bank = transpose_words(words[:, u, :, :])
+                group_words(bank, x1_group[:, u * 1024 : (u + 1) * 1024])
+            x2_group = grouped.tile([P, 2 * P * PACK], BF16, align_bytes=64)
+            bank = transpose_words(x2_half[:].bitcast(F32))
+            group_words(bank, x2_group[:])
+            x1_cols = slice(half * 512, (half + 1) * 512)
+            x2_cols = slice(1024 + half * 256, 1024 + (half + 1) * 256)
+            return [
+                (x1_group[:], x_codes[b][:, x1_cols], x_scales[b][:, x1_cols]),
+                (x2_group[:], x_codes[b][:, x2_cols], x_scales[b][:, x2_cols]),
+            ]
+
+        def score_columns(b, j):
+            q_el = q_turned[b][:].bitcast(BF16).rearrange("p u (l e) -> p u l e", e=2)
+            k_el = k_turned[b][:].bitcast(BF16).rearrange("p u (l e) -> p u l e", e=2)
+            unit = QUARTERS * b + j
+            a_rows = scores.tile([P, L1], F32)
+            a_turned[(b, j)] = a_rows
+            for h in range(2):
+                bank = psum.tile([P, BANK], F32, tag="bank")
+                for t in range(PACK):
+                    u, e = divmod(t, 2)
+                    nc.tensor.matmul(
+                        bank[:],
+                        lhsT=k_el[:, u, j * P : (j + 1) * P, e],
+                        rhs=q_el[:, u, h * BANK : (h + 1) * BANK, e],
+                        start=(t == 0),
+                        stop=(t == PACK - 1),
+                    )
+                nc.vector.tensor_scalar(
+                    out=a_rows[:, h * BANK : (h + 1) * BANK],
+                    in0=bank[:],
+                    scalar1=mask_term[:, unit : unit + 1],
+                    scalar2=None,
+                    op0=ALU.add,
+                    op1=ALU.max,
+                    accum_out=col_max[:, 2 * unit + h : 2 * unit + h + 1],
+                )
+            nc.vector.tensor_scalar(
+                out=col_shift[:, unit : unit + 1],
+                in0=col_max[:, 2 * unit : 2 * unit + 1],
+                scalar1=col_max[:, 2 * unit + 1 : 2 * unit + 2],
+                scalar2=-SCALE,
+                op0=ALU.max,
+                op1=ALU.mult,
+            )
+
+        def exp_columns(b, j):
+            unit = QUARTERS * b + j
+            e1_rows = exps.tile([P, 2, 512], BF16)
+            nc.scalar.activation(
+                out=e1_rows[:].rearrange("p g l -> p (g l)"),
+                in_=a_turned[(b, j)][:],
+                func=ACT.Exp,
+                bias=col_shift[:, unit : unit + 1],
+                scale=SCALE,
+                accum_out=col_sum[:, unit : unit + 1],
+            )
+            return e1_rows
+
+        def transpose_exp(rows, which, steps_kept):
+            bank = transpose_words(rows[:].bitcast(F32))
+            e_group = grouped.tile([P, 2 * P * PACK], BF16, bufs=4, align_bytes=64)
+            group_words(bank, e_group[:])
+            bufs = steps_kept + 2
+            codes = packed.tile([P, 2 * P], U32, tag=which + "_codes", bufs=bufs, align_bytes=64)
+            scales = packed.tile([P, 2 * P], U8, tag=which + "_scales", bufs=bufs, align_bytes=64)
+            return codes, scales, (e_group[:], codes[:], scales[:])
+
+        def score_rows(b, pair):
+            banks = []
+            first = 2 * (QUARTERS * b + pair)
+            for c in range(2):
+                i = 2 * pair + c
+                bank = psum.tile([P, L2], F32, tag="bank")
+                for j in range(4):
+                    nc.tensor.transpose(
+                        bank[:, j * P : (j + 1) * P],
+                        a_turned[(b, j)][:, i * P : (i + 1) * P],
+                        ident[:],
+                    )
+                nc.vector.tensor_reduce(
+                    out=row_max[:, first + c : first + c + 1], in_=bank[:], op=ALU.max, axis=AXIS.X
+                )
+                banks.append(bank)
+            nc.vector.tensor_scalar_mul(
+                out=row_shift[:, first : first + 2],
+                in0=row_max[:, first : first + 2],
+                scalar1=-SCALE,
+            )
+            return banks
+
+        def exp_rows(b, pair, banks):
+            first = 2 * (QUARTERS * b + pair)
+            e2_pair = exps.tile([P, 2, L2], BF16)
+            e2_rows[(b, pair)] = e2_pair
+            for c in range(2):
+                nc.scalar.activation(
+                    out=e2_pair[:, c, :],
+                    in_=banks[c][:],
+                    func=ACT.Exp,
+                    bias=row_shift[:, first + c : first + c + 1],
+                    scale=SCALE,
+                    accum_out=row_sum[:, first + c : first + c + 1],
+                )
+
+        def project(b, block):
+            if block == 0:
+                codes = packed.tile([P, 3, D], U32, tag="v_codes", align_bytes=64)
+                scales = packed.tile([P, 3, D], U8, tag="v_scales", align_bytes=64)
+                v_codes[b] = codes
+                v_scales[b] = scales
+            cols = slice(block * P, (block + 1) * P)
+            v_group = grouped.tile([P, 3, P, PACK], BF16, align_bytes=64)
+            calls = []
+            for w in range(3):
+                bank = psum.tile([P, PACK, P], F32, tag="bank")
+                for t in range(PACK):
+                    rows = slice((PACK * w + t) * P, (PACK * w + t + 1) * P)
+                    nc.tensor.matmul_mx(
+                        out=bank[:, t, :],
+                        lhsT=x_codes[b][:, rows].bitcast(FP8X4),
+                        lhsT_scale=x_scales[b][:, rows],
+                        rhs=wv_codes[:, cols].bitcast(FP8X4),
+                        rhs_scale=wv_scales[:, cols],
+                        start=True,
+                        stop=True,
+                    )
+                nc.vector.tensor_tensor(
+                    out=v_group[:, w, :, :],
+                    in0=bank[:].rearrange("p t d -> p d t"),
+                    in1=bias[:, cols].unsqueeze(2).to_broadcast([P, P, PACK]),
+                    op=ALU.add,
+                )
+                calls.append(
+                    (
+                        v_group[:, w, :, :].rearrange("p d t -> p (d t)"),
+                        v_codes[b][:, w, cols],
+                        v_scales[b][:, w, cols],
+                    )
+                )
+            return calls
+
+        def output_weights(b, quarter):
+            unit = QUARTERS * b + quarter
+            nc.vector.reciprocal(col_weight[:, unit : unit + 1], col_sum[:, unit : unit + 1])
+            nc.vector.tensor_mul(
+                out=col_weight[:, unit : unit + 1],
+                in0=col_weight[:, unit : unit + 1],
+                in1=keep[:, unit : unit + 1],
+            )
+            nc.vector.reciprocal(
+                row_weight[:, 2 * unit : 2 * unit + 2], row_sum[:, 2 * unit : 2 * unit + 2]
+            )
+
+        def x1_mid_rows(b, j):
+            unit = QUARTERS * b + j
+            bank = psum.tile([P, D], F32, tag="bank")
+            for g in range(2):
+                cols = slice(g * P, (g + 1) * P)
+                nc.tensor.matmul_mx(
+                    out=bank[:],
+                    lhsT=e1_codes[(b, j)][:, cols].bitcast(FP8X4),
+                    lhsT_scale=e1_scales[(b, j)][:, cols],
+                    rhs=v_codes[b][:, g, :].bitcast(FP8X4),
+                    rhs_scale=v_scales[b][:, g, :],
+                    start=(g == 0),
+                    stop=(g == 1),
+                )
+            mid = results.tile([P, D], F32)
+            nc.scalar.activation(
+                out=mid[:], in_=bank[:], func=ACT.Copy, scale=col_weight[:, unit : unit + 1]
+            )
+            nc.sync.dma_start(out=out_1[b, j * P : (j + 1) * P, :], in_=mid[:])
+
+        def x2_out_rows(b, pair):
+            first = 2 * (QUARTERS * b + pair)
+            both = results.tile([P, 2, D], F32)
+            for c in range(2):
+                cols = slice(c * P, (c + 1) * P)
+                bank = psum.tile([P, D], F32, tag="bank")
+                nc.tensor.matmul_mx(
+                    out=bank[:],
+                    lhsT=e2_codes[(b, pair)][:, cols].bitcast(FP8X4),
+                    lhsT_scale=e2_scales[(b, pair)][:, cols],
+                    rhs=v_codes[b][:, 2, :].bitcast(FP8X4),
+                    rhs_scale=v_scales[b][:, 2, :],
+                    start=True,
+                    stop=True,
+                )
+                weight = row_weight[:, first + c : first + c + 1]
+                if c == 0:
+                    nc.scalar.activation(out=both[:, c, :], in_=bank[:], func=ACT.Copy, scale=weight)
+                else:
+                    nc.vector.tensor_scalar_mul(out=both[:, c, :], in0=bank[:], scalar1=weight)
+            rows = out_0[b, pair * 256 : (pair + 1) * 256, :]
+            nc.sync.dma_start(out=rows.rearrange("(c m) d -> m c d", m=P), in_=both[:])
+
+        to_quantise = []
+        for step in range(STEPS):
+            for group, codes, scales in to_quantise:
+                nc.vector.quantize_mx(out=codes.bitcast(FP8X4), scales=scales, in_=group)
+            to_quantise = []
+            outputs = unit_of(step, AT_OUTPUTS)
+            if outputs:
+                output_weights(*outputs)
+
+            e1_unit = unit_of(step, AT_E1)
+            if e1_unit:
+                e1_rows = exp_columns(*e1_unit)
+
+            unit = unit_of(step, AT_SCORES)
+            if unit:
+                score_columns(*unit)
+
+            unit = unit_of(step, AT_INPUTS)
+            if unit:
+                b, quarter = unit
+                if quarter < 2:
+                    transpose_q_k(b, quarter)
+                else:
+                    to_quantise.extend(transpose_x(b, quarter - 2))
+                if step + LOAD_AHEAD < UNITS:
+                    load(step + LOAD_AHEAD)
+            rows_unit = unit_of(step, AT_ROWS)
+            if rows_unit:
+                banks = score_rows(*rows_unit)
+            if e1_unit:
+                e1_codes[e1_unit], e1_scales[e1_unit], call = transpose_exp(
+                    e1_rows, "e1", AT_OUTPUTS - AT_E1
+                )
+                to_quantise.append(call)
+            unit = unit_of(step, AT_E2)
+            if unit:
+                e2_codes[unit], e2_scales[unit], call = transpose_exp(
+                    e2_rows[unit], "e2", AT_OUTPUTS - AT_E2
+                )
+                to_quantise.append(call)
+            if rows_unit:
+                exp_rows(rows_unit[0], rows_unit[1], banks)
+
+            unit = unit_of(step, AT_PROJECT)
+            if unit:
+                to_quantise.extend(project(*unit))
+            if outputs:
+                x1_mid_rows(*outputs)
+                x2_out_rows(*outputs)

@@ -73,12 +73,10 @@ def tile_coattention_pa_t_kernel(tc, q, k, x1, x2, mask, Wv, bv, out_0, out_1):
 
         col_max = const.tile([P, 2 * UNITS], F32)
         col_shift = const.tile([P, UNITS], F32)
-        col_sum = const.tile([P, UNITS], F32)
-        col_weight = const.tile([P, UNITS], F32)
         row_max = const.tile([P, 2 * UNITS], F32)
         row_shift = const.tile([P, 2 * UNITS], F32)
-        row_sum = const.tile([P, 2 * UNITS], F32)
-        row_weight = const.tile([P, 2 * UNITS], F32)
+        sums = const.tile([P, UNITS, 3], F32)
+        weights = const.tile([P, UNITS, 3], F32)
 
         loaded = {}
 
@@ -104,15 +102,17 @@ def tile_coattention_pa_t_kernel(tc, q, k, x1, x2, mask, Wv, bv, out_0, out_1):
                 nc.sync.dma_start(out=x2_half[:], in_=rows.rearrange("(m e) d -> m e d", e=2))
                 loaded[n] = (x1_half, x2_half)
 
-        wv_rows = const.tile([P, 4, D], BF16)
-        nc.scalar.dma_start(out=wv_rows[:], in_=Wv.rearrange("(c m) d -> m c d", m=P))
         mask_rows = const.tile([P, P], BF16)
         nc.vector.memset(mask_rows[:], 0.0)
         nc.scalar.dma_start(
             out=mask_rows[0:UNITS, :], in_=mask.rearrange("b (j p) -> (b j) p", p=P)
         )
-        for n in range(4):
-            load(n)
+        load(0)
+        load(1)
+        wv_rows = const.tile([P, 4, D], BF16)
+        nc.sync.dma_start(out=wv_rows[:], in_=Wv.rearrange("(c m) d -> m c d", m=P))
+        load(2)
+        load(3)
         bias = const.tile([P, D], BF16)
         nc.sync.dma_start(out=bias[:], in_=bv.partition_broadcast(P))
         for n in range(4, LOAD_AHEAD):
@@ -132,13 +132,13 @@ def tile_coattention_pa_t_kernel(tc, q, k, x1, x2, mask, Wv, bv, out_0, out_1):
         wv_group = const.tile([P, D * PACK], BF16, align_bytes=64)
         wv_codes = const.tile([P, D], U32, align_bytes=64)
         wv_scales = const.tile([P, D], U8, align_bytes=64)
-        wv_words = wv_rows[:].bitcast(F32)
-        for pair in range(2):
-            bank = transpose_words(wv_words[:, 2 * pair : 2 * pair + 2, :])
-            group_words(bank, wv_group[:, pair * 1024 : (pair + 1) * 1024])
-        nc.vector.quantize_mx(
-            out=wv_codes[:].bitcast(FP8X4), scales=wv_scales[:], in_=wv_group[:]
-        )
+
+        def transpose_wv():
+            words = wv_rows[:].bitcast(F32)
+            for pair in range(2):
+                bank = transpose_words(words[:, 2 * pair : 2 * pair + 2, :])
+                group_words(bank, wv_group[:, pair * 1024 : (pair + 1) * 1024])
+            return (wv_group[:], wv_codes[:], wv_scales[:])
 
         q_turned, k_turned = {}, {}
         x_codes, x_scales = {}, {}
@@ -220,7 +220,7 @@ def tile_coattention_pa_t_kernel(tc, q, k, x1, x2, mask, Wv, bv, out_0, out_1):
                     op1=ALU.max,
                     accum_out=col_max[:, 2 * unit + h : 2 * unit + h + 1],
                 )
-            nc.vector.tensor_scalar(
+            nc.gpsimd.tensor_scalar(
                 out=col_shift[:, unit : unit + 1],
                 in0=col_max[:, 2 * unit : 2 * unit + 1],
                 scalar1=col_max[:, 2 * unit + 1 : 2 * unit + 2],
@@ -238,7 +238,7 @@ def tile_coattention_pa_t_kernel(tc, q, k, x1, x2, mask, Wv, bv, out_0, out_1):
                 func=ACT.Exp,
                 bias=col_shift[:, unit : unit + 1],
                 scale=SCALE,
-                accum_out=col_sum[:, unit : unit + 1],
+                accum_out=sums[:, unit, 0:1],
             )
             return e1_rows
 
@@ -275,7 +275,8 @@ def tile_coattention_pa_t_kernel(tc, q, k, x1, x2, mask, Wv, bv, out_0, out_1):
             return banks
 
         def exp_rows(b, pair, banks):
-            first = 2 * (QUARTERS * b + pair)
+            unit = QUARTERS * b + pair
+            first = 2 * unit
             e2_pair = exps.tile([P, 2, L2], BF16)
             e2_rows[(b, pair)] = e2_pair
             for c in range(2):
@@ -285,7 +286,7 @@ def tile_coattention_pa_t_kernel(tc, q, k, x1, x2, mask, Wv, bv, out_0, out_1):
                     func=ACT.Exp,
                     bias=row_shift[:, first + c : first + c + 1],
                     scale=SCALE,
-                    accum_out=row_sum[:, first + c : first + c + 1],
+                    accum_out=sums[:, unit, 1 + c : 2 + c],
                 )
 
         def project(b, block):
@@ -327,15 +328,7 @@ def tile_coattention_pa_t_kernel(tc, q, k, x1, x2, mask, Wv, bv, out_0, out_1):
 
         def output_weights(b, quarter):
             unit = QUARTERS * b + quarter
-            nc.vector.reciprocal(col_weight[:, unit : unit + 1], col_sum[:, unit : unit + 1])
-            nc.vector.tensor_mul(
-                out=col_weight[:, unit : unit + 1],
-                in0=col_weight[:, unit : unit + 1],
-                in1=keep[:, unit : unit + 1],
-            )
-            nc.vector.reciprocal(
-                row_weight[:, 2 * unit : 2 * unit + 2], row_sum[:, 2 * unit : 2 * unit + 2]
-            )
+            nc.vector.reciprocal(weights[:, unit, :], sums[:, unit, :])
 
         def x1_mid_rows(b, j):
             unit = QUARTERS * b + j
@@ -352,13 +345,18 @@ def tile_coattention_pa_t_kernel(tc, q, k, x1, x2, mask, Wv, bv, out_0, out_1):
                     stop=(g == 1),
                 )
             mid = results.tile([P, D], F32)
-            nc.scalar.activation(
-                out=mid[:], in_=bank[:], func=ACT.Copy, scale=col_weight[:, unit : unit + 1]
+            nc.vector.tensor_scalar(
+                out=mid[:],
+                in0=bank[:],
+                scalar1=weights[:, unit, 0:1],
+                scalar2=keep[:, unit : unit + 1],
+                op0=ALU.mult,
+                op1=ALU.mult,
             )
             nc.sync.dma_start(out=out_1[b, j * P : (j + 1) * P, :], in_=mid[:])
 
         def x2_out_rows(b, pair):
-            first = 2 * (QUARTERS * b + pair)
+            unit = QUARTERS * b + pair
             both = results.tile([P, 2, D], F32)
             for c in range(2):
                 cols = slice(c * P, (c + 1) * P)
@@ -372,11 +370,12 @@ def tile_coattention_pa_t_kernel(tc, q, k, x1, x2, mask, Wv, bv, out_0, out_1):
                     start=True,
                     stop=True,
                 )
-                weight = row_weight[:, first + c : first + c + 1]
-                if c == 0:
-                    nc.scalar.activation(out=both[:, c, :], in_=bank[:], func=ACT.Copy, scale=weight)
-                else:
-                    nc.vector.tensor_scalar_mul(out=both[:, c, :], in0=bank[:], scalar1=weight)
+                nc.scalar.activation(
+                    out=both[:, c, :],
+                    in_=bank[:],
+                    func=ACT.Copy,
+                    scale=weights[:, unit, 1 + c : 2 + c],
+                )
             rows = out_0[b, pair * 256 : (pair + 1) * 256, :]
             nc.sync.dma_start(out=rows.rearrange("(c m) d -> m c d", m=P), in_=both[:])
 
@@ -406,6 +405,8 @@ def tile_coattention_pa_t_kernel(tc, q, k, x1, x2, mask, Wv, bv, out_0, out_1):
                     to_quantise.extend(transpose_x(b, quarter - 2))
                 if step + LOAD_AHEAD < UNITS:
                     load(step + LOAD_AHEAD)
+            if step == AT_PROJECT - 1:
+                to_quantise.append(transpose_wv())
             rows_unit = unit_of(step, AT_ROWS)
             if rows_unit:
                 banks = score_rows(*rows_unit)

@@ -32,6 +32,7 @@ AT_ROWS = 5
 AT_E2 = 6
 AT_OUTPUTS = 8
 STEPS = UNITS + AT_OUTPUTS
+PIECES = 3
 LOAD_AHEAD = 8
 
 
@@ -39,7 +40,7 @@ def tile_coattention_pa_t_kernel(tc, q, k, x1, x2, mask, Wv, bv, out_0, out_1):
     nc = tc.nc
     with ExitStack() as ctx:
         const = ctx.enter_context(tc.tile_pool(name="const", bufs=1))
-        inputs = ctx.enter_context(tc.tile_pool(name="inputs", bufs=4))
+        inputs = ctx.enter_context(tc.tile_pool(name="inputs", bufs=PIECES * LOAD_AHEAD))
         turned = ctx.enter_context(tc.tile_pool(name="turned", bufs=2))
         grouped = ctx.enter_context(tc.tile_pool(name="grouped", bufs=2))
         packed = ctx.enter_context(tc.tile_pool(name="packed", bufs=2))
@@ -83,32 +84,25 @@ def tile_coattention_pa_t_kernel(tc, q, k, x1, x2, mask, Wv, bv, out_0, out_1):
         def load(n):
             b, quarter = divmod(n, QUARTERS)
             half = quarter % 2
-            if quarter < 2:
-                q_half = inputs.tile([P, 4, D], BF16)
-                rows = q[b, half * 512 : (half + 1) * 512, :]
-                nc.sync.dma_start(out=q_half[:], in_=rows.rearrange("(c m) d -> m c d", m=P))
-                k_half = inputs.tile([P, 2, D], BF16)
-                rows = k[b, half * 256 : (half + 1) * 256, :]
-                nc.sync.dma_start(out=k_half[:], in_=rows.rearrange("(c m) d -> m c d", m=P))
-                loaded[n] = (q_half, k_half)
-            else:
-                x1_half = inputs.tile([P, 2, 2, D], BF16)
-                rows = x1[b, half * 512 : (half + 1) * 512, :]
-                nc.sync.dma_start(
-                    out=x1_half[:], in_=rows.rearrange("(u m e) d -> m u e d", u=2, e=2)
-                )
-                x2_half = inputs.tile([P, 2, D], BF16)
-                rows = x2[b, half * 256 : (half + 1) * 256, :]
-                nc.sync.dma_start(out=x2_half[:], in_=rows.rearrange("(m e) d -> m e d", e=2))
-                loaded[n] = (x1_half, x2_half)
+            for piece in range(PIECES):
+                long_one, short_one = (q, k) if quarter < 2 else (x1, x2)
+                source = long_one if piece < 2 else short_one
+                first = (2 * half + piece) * 256 if piece < 2 else half * 256
+                rows = source[b, first : first + 256, :]
+                tile_in = inputs.tile([P, 2, D], BF16)
+                if quarter < 2:
+                    nc.sync.dma_start(out=tile_in[:], in_=rows.rearrange("(c m) d -> m c d", m=P))
+                else:
+                    nc.sync.dma_start(out=tile_in[:], in_=rows.rearrange("(m e) d -> m e d", e=2))
+                loaded[(n, piece)] = tile_in
 
-        mask_rows = const.tile([P, P], BF16)
-        nc.vector.memset(mask_rows[:], 0.0)
-        nc.scalar.dma_start(
-            out=mask_rows[0:UNITS, :], in_=mask.rearrange("b (j p) -> (b j) p", p=P)
-        )
         load(0)
         load(1)
+        mask_rows = const.tile([P, P], BF16)
+        nc.vector.memset(mask_rows[:], 0.0)
+        nc.sync.dma_start(
+            out=mask_rows[0:UNITS, :], in_=mask.rearrange("b (j p) -> (b j) p", p=P)
+        )
         wv_rows = const.tile([P, 4, D], BF16)
         nc.sync.dma_start(out=wv_rows[:], in_=Wv.rearrange("(c m) d -> m c d", m=P))
         load(2)
@@ -118,16 +112,23 @@ def tile_coattention_pa_t_kernel(tc, q, k, x1, x2, mask, Wv, bv, out_0, out_1):
         for n in range(4, LOAD_AHEAD):
             load(n)
 
-        mask_f32 = const.tile([P, P], F32)
-        nc.vector.tensor_copy(out=mask_f32[:], in_=mask_rows[:])
-        mask_bank = psum.tile([P, P], F32, tag="bank")
-        nc.tensor.transpose(mask_bank[:], mask_f32[:], ident[:])
         keep = const.tile([P, UNITS], F32)
-        nc.vector.tensor_copy(out=keep[:], in_=mask_bank[:, 0:UNITS])
         mask_term = const.tile([P, UNITS], F32)
-        nc.vector.tensor_scalar(
-            out=mask_term[:], in0=keep[:], scalar1=-1.0, scalar2=MASKED, op0=ALU.add, op1=ALU.mult
-        )
+
+        def transpose_mask():
+            mask_f32 = const.tile([P, P], F32)
+            nc.vector.tensor_copy(out=mask_f32[:], in_=mask_rows[:])
+            mask_bank = psum.tile([P, P], F32, tag="bank")
+            nc.tensor.transpose(mask_bank[:], mask_f32[:], ident[:])
+            nc.vector.tensor_copy(out=keep[:], in_=mask_bank[:, 0:UNITS])
+            nc.vector.tensor_scalar(
+                out=mask_term[:],
+                in0=keep[:],
+                scalar1=-1.0,
+                scalar2=MASKED,
+                op0=ALU.add,
+                op1=ALU.mult,
+            )
 
         wv_group = const.tile([P, D * PACK], BF16, align_bytes=64)
         wv_codes = const.tile([P, D], U32, align_bytes=64)
@@ -141,6 +142,7 @@ def tile_coattention_pa_t_kernel(tc, q, k, x1, x2, mask, Wv, bv, out_0, out_1):
             return (wv_group[:], wv_codes[:], wv_scales[:])
 
         q_turned, k_turned = {}, {}
+        x_group = {}
         x_codes, x_scales = {}, {}
         v_codes, v_scales = {}, {}
         a_turned = {}
@@ -148,78 +150,74 @@ def tile_coattention_pa_t_kernel(tc, q, k, x1, x2, mask, Wv, bv, out_0, out_1):
         e2_rows = {}
         e2_codes, e2_scales = {}, {}
 
-        def transpose_q_k(b, half):
-            q_half, k_half = loaded[QUARTERS * b + half]
-            if half == 0:
+        def start_input(b, quarter):
+            half = quarter % 2
+            if quarter == 0:
                 q_words = turned.tile([P, 2, L1], F32)
                 k_words = turned.tile([P, 2, L2], F32)
                 q_turned[b] = q_words
                 k_turned[b] = k_words
-            words = q_half[:].bitcast(F32)
-            for pair in range(2):
-                bank = transpose_words(words[:, 2 * pair : 2 * pair + 2, :])
-                first = half * 512 + pair * 256
-                nc.scalar.copy(
-                    out=q_turned[b][:, :, first : first + 256].rearrange(
-                        "p u (c r) -> p u c r", c=2
-                    ),
-                    in_=bank[:].rearrange("p c u r -> p u c r"),
-                )
-            bank = transpose_words(k_half[:].bitcast(F32))
-            first = half * 256
-            nc.scalar.copy(
-                out=k_turned[b][:, :, first : first + 256].rearrange("p u (c r) -> p u c r", c=2),
-                in_=bank[:].rearrange("p c u r -> p u c r"),
-            )
-
-        def transpose_x(b, half):
-            x1_half, x2_half = loaded[QUARTERS * b + 2 + half]
-            if half == 0:
+            if quarter == 2:
                 codes = packed.tile([P, 12 * P], U32, tag="x_codes", align_bytes=64)
                 scales = packed.tile([P, 12 * P], U8, tag="x_scales", align_bytes=64)
                 x_codes[b] = codes
                 x_scales[b] = scales
-            x1_group = grouped.tile([P, 4 * P * PACK], BF16, align_bytes=64)
-            words = x1_half[:].bitcast(F32)
-            for u in range(2):
-                bank = transpose_words(words[:, u, :, :])
-                group_words(bank, x1_group[:, u * 1024 : (u + 1) * 1024])
-            x2_group = grouped.tile([P, 2 * P * PACK], BF16, align_bytes=64)
-            bank = transpose_words(x2_half[:].bitcast(F32))
-            group_words(bank, x2_group[:])
+            if quarter < 2:
+                return []
+            group = grouped.tile([P, PIECES * 2 * P * PACK], BF16, tag="x_group", align_bytes=64)
+            x_group[b] = group
             x1_cols = slice(half * 512, (half + 1) * 512)
             x2_cols = slice(1024 + half * 256, 1024 + (half + 1) * 256)
             return [
-                (x1_group[:], x_codes[b][:, x1_cols], x_scales[b][:, x1_cols]),
-                (x2_group[:], x_codes[b][:, x2_cols], x_scales[b][:, x2_cols]),
+                (group[:, 0:2048], x_codes[b][:, x1_cols], x_scales[b][:, x1_cols]),
+                (group[:, 2048:3072], x_codes[b][:, x2_cols], x_scales[b][:, x2_cols]),
             ]
 
-        def score_columns(b, j):
+        def transpose_input(b, quarter, piece):
+            half = quarter % 2
+            bank = transpose_words(loaded[(QUARTERS * b + quarter, piece)][:].bitcast(F32))
+            if quarter < 2:
+                if piece < 2:
+                    first = (2 * half + piece) * 256
+                    target = q_turned[b][:, :, first : first + 256]
+                else:
+                    target = k_turned[b][:, :, half * 256 : (half + 1) * 256]
+                nc.scalar.copy(
+                    out=target.rearrange("p u (c r) -> p u c r", c=2),
+                    in_=bank[:].rearrange("p c u r -> p u c r"),
+                )
+            else:
+                group_words(bank, x_group[b][:, piece * 1024 : (piece + 1) * 1024])
+
+        def score_bank(b, j, h):
             q_el = q_turned[b][:].bitcast(BF16).rearrange("p u (l e) -> p u l e", e=2)
             k_el = k_turned[b][:].bitcast(BF16).rearrange("p u (l e) -> p u l e", e=2)
             unit = QUARTERS * b + j
-            a_rows = scores.tile([P, L1], F32)
-            a_turned[(b, j)] = a_rows
-            for h in range(2):
-                bank = psum.tile([P, BANK], F32, tag="bank")
-                for t in range(PACK):
-                    u, e = divmod(t, 2)
-                    nc.tensor.matmul(
-                        bank[:],
-                        lhsT=k_el[:, u, j * P : (j + 1) * P, e],
-                        rhs=q_el[:, u, h * BANK : (h + 1) * BANK, e],
-                        start=(t == 0),
-                        stop=(t == PACK - 1),
-                    )
-                nc.vector.tensor_scalar(
-                    out=a_rows[:, h * BANK : (h + 1) * BANK],
-                    in0=bank[:],
-                    scalar1=mask_term[:, unit : unit + 1],
-                    scalar2=None,
-                    op0=ALU.add,
-                    op1=ALU.max,
-                    accum_out=col_max[:, 2 * unit + h : 2 * unit + h + 1],
+            if h == 0:
+                a_rows = scores.tile([P, L1], F32)
+                a_turned[(b, j)] = a_rows
+            bank = psum.tile([P, BANK], F32, tag="bank")
+            for t in range(PACK):
+                u, e = divmod(t, 2)
+                nc.tensor.matmul(
+                    bank[:],
+                    lhsT=k_el[:, u, j * P : (j + 1) * P, e],
+                    rhs=q_el[:, u, h * BANK : (h + 1) * BANK, e],
+                    start=(t == 0),
+                    stop=(t == PACK - 1),
                 )
+            nc.vector.tensor_scalar(
+                out=a_turned[(b, j)][:, h * BANK : (h + 1) * BANK],
+                in0=bank[:],
+                scalar1=mask_term[:, unit : unit + 1],
+                scalar2=None,
+                op0=ALU.add,
+                op1=ALU.max,
+                accum_out=col_max[:, 2 * unit + h : 2 * unit + h + 1],
+            )
+
+        def column_shift(b, j):
+            unit = QUARTERS * b + j
             nc.gpsimd.tensor_scalar(
                 out=col_shift[:, unit : unit + 1],
                 in0=col_max[:, 2 * unit : 2 * unit + 1],
@@ -392,19 +390,22 @@ def tile_coattention_pa_t_kernel(tc, q, k, x1, x2, mask, Wv, bv, out_0, out_1):
             if e1_unit:
                 e1_rows = exp_columns(*e1_unit)
 
-            unit = unit_of(step, AT_SCORES)
-            if unit:
-                score_columns(*unit)
+            scores_unit = unit_of(step, AT_SCORES)
+            inputs_unit = unit_of(step, AT_INPUTS)
+            if inputs_unit:
+                to_quantise.extend(start_input(*inputs_unit))
+            for piece in range(PIECES):
+                if scores_unit and piece < 2:
+                    score_bank(scores_unit[0], scores_unit[1], piece)
+                if inputs_unit:
+                    transpose_input(inputs_unit[0], inputs_unit[1], piece)
+            if scores_unit:
+                column_shift(*scores_unit)
+            if inputs_unit and step + LOAD_AHEAD < UNITS:
+                load(step + LOAD_AHEAD)
 
-            unit = unit_of(step, AT_INPUTS)
-            if unit:
-                b, quarter = unit
-                if quarter < 2:
-                    transpose_q_k(b, quarter)
-                else:
-                    to_quantise.extend(transpose_x(b, quarter - 2))
-                if step + LOAD_AHEAD < UNITS:
-                    load(step + LOAD_AHEAD)
+            if step == AT_SCORES - 1:
+                transpose_mask()
             if step == AT_PROJECT - 1:
                 to_quantise.append(transpose_wv())
             rows_unit = unit_of(step, AT_ROWS)

@@ -51,7 +51,7 @@ def tile_coattention_pa_t_kernel(tc, q, k, x1, x2, mask, Wv, bv, out_0, out_1):
         ctx.enter_context(tc.manual_schedule())
 
         def transpose_words(words):
-            bank = psum.tile([P, 2, 2, P], F32, tag="bank")
+            bank = psum.tile([P, 2, 2, P], F32, tag="bank", bufs=6)
             for block in range(2):
                 for u in range(2):
                     nc.tensor.transpose(
@@ -118,7 +118,7 @@ def tile_coattention_pa_t_kernel(tc, q, k, x1, x2, mask, Wv, bv, out_0, out_1):
         def transpose_mask():
             mask_f32 = const.tile([P, P], F32)
             nc.vector.tensor_copy(out=mask_f32[:], in_=mask_rows[:])
-            mask_bank = psum.tile([P, P], F32, tag="bank")
+            mask_bank = psum.tile([P, P], F32, tag="bank", bufs=6)
             nc.tensor.transpose(mask_bank[:], mask_f32[:], ident[:])
             nc.vector.tensor_copy(out=keep[:], in_=mask_bank[:, 0:UNITS])
             nc.vector.tensor_scalar(
@@ -196,7 +196,7 @@ def tile_coattention_pa_t_kernel(tc, q, k, x1, x2, mask, Wv, bv, out_0, out_1):
             if h == 0:
                 a_rows = scores.tile([P, L1], F32)
                 a_turned[(b, j)] = a_rows
-            bank = psum.tile([P, BANK], F32, tag="bank")
+            bank = psum.tile([P, BANK], F32, tag="bank", bufs=6)
             for t in range(PACK):
                 u, e = divmod(t, 2)
                 nc.tensor.matmul(
@@ -254,7 +254,7 @@ def tile_coattention_pa_t_kernel(tc, q, k, x1, x2, mask, Wv, bv, out_0, out_1):
             first = 2 * (QUARTERS * b + pair)
             for c in range(2):
                 i = 2 * pair + c
-                bank = psum.tile([P, L2], F32, tag="bank")
+                bank = psum.tile([P, L2], F32, tag="rows", bufs=2)
                 for j in range(4):
                     nc.tensor.transpose(
                         bank[:, j * P : (j + 1) * P],
@@ -297,7 +297,7 @@ def tile_coattention_pa_t_kernel(tc, q, k, x1, x2, mask, Wv, bv, out_0, out_1):
             v_group = grouped.tile([P, 3, P, PACK], BF16, align_bytes=64)
             calls = []
             for w in range(3):
-                bank = psum.tile([P, PACK, P], F32, tag="bank")
+                bank = psum.tile([P, PACK, P], F32, tag="bank", bufs=6)
                 for t in range(PACK):
                     rows = slice((PACK * w + t) * P, (PACK * w + t + 1) * P)
                     nc.tensor.matmul_mx(
@@ -330,7 +330,7 @@ def tile_coattention_pa_t_kernel(tc, q, k, x1, x2, mask, Wv, bv, out_0, out_1):
 
         def x1_mid_rows(b, j):
             unit = QUARTERS * b + j
-            bank = psum.tile([P, D], F32, tag="bank")
+            bank = psum.tile([P, D], F32, tag="bank", bufs=6)
             for g in range(2):
                 cols = slice(g * P, (g + 1) * P)
                 nc.tensor.matmul_mx(
@@ -358,7 +358,7 @@ def tile_coattention_pa_t_kernel(tc, q, k, x1, x2, mask, Wv, bv, out_0, out_1):
             both = results.tile([P, 2, D], F32)
             for c in range(2):
                 cols = slice(c * P, (c + 1) * P)
-                bank = psum.tile([P, D], F32, tag="bank")
+                bank = psum.tile([P, D], F32, tag="bank", bufs=6)
                 nc.tensor.matmul_mx(
                     out=bank[:],
                     lhsT=e2_codes[(b, pair)][:, cols].bitcast(FP8X4),

@@ -26,11 +26,11 @@ QUARTERS = 4
 UNITS = QUARTERS * B
 AT_INPUTS = 0
 AT_SCORES = 2
-AT_E1 = 3
-AT_PROJECT = 4
-AT_ROWS = 5
-AT_E2 = 6
-AT_OUTPUTS = 8
+AT_E1 = 5
+AT_PROJECT = 3
+AT_ROWS = 4
+AT_E2 = 5
+AT_OUTPUTS = 7
 STEPS = UNITS + AT_OUTPUTS
 PIECES = 3
 LOAD_AHEAD = 8
@@ -78,6 +78,7 @@ def tile_coattention_pa_t_kernel(tc, q, k, x1, x2, mask, Wv, bv, out_0, out_1):
         row_shift = const.tile([P, 2 * UNITS], F32)
         sums = const.tile([P, UNITS, 3], F32)
         weights = const.tile([P, UNITS, 3], F32)
+        mid_weights = const.tile([P, UNITS], F32)
 
         loaded = {}
 
@@ -145,6 +146,7 @@ def tile_coattention_pa_t_kernel(tc, q, k, x1, x2, mask, Wv, bv, out_0, out_1):
         x_group = {}
         x_codes, x_scales = {}, {}
         v_codes, v_scales = {}, {}
+        v_group = {}
         a_turned = {}
         e1_codes, e1_scales = {}, {}
         e2_rows = {}
@@ -240,14 +242,29 @@ def tile_coattention_pa_t_kernel(tc, q, k, x1, x2, mask, Wv, bv, out_0, out_1):
             )
             return e1_rows
 
-        def transpose_exp(rows, which, steps_kept):
+        def start_exponentials(e1_unit, e2_unit):
+            units = [(e1_codes, e1_scales, e1_unit), (e2_codes, e2_scales, e2_unit)]
+            units = [entry for entry in units if entry[2]]
+            count = len(units)
+            bufs = AT_OUTPUTS - AT_E1 + 2
+            group = grouped.tile(
+                [P, count, 2 * P * PACK], BF16, tag="e_group%d" % count, align_bytes=64
+            )
+            codes = packed.tile(
+                [P, count, 2 * P], U32, tag="e_codes%d" % count, bufs=bufs, align_bytes=64
+            )
+            scales = packed.tile(
+                [P, count, 2 * P], U8, tag="e_scales%d" % count, bufs=bufs, align_bytes=64
+            )
+            for n, (all_codes, all_scales, unit) in enumerate(units):
+                all_codes[unit] = codes[:, n, :]
+                all_scales[unit] = scales[:, n, :]
+            call = tuple(part[:].rearrange("p n w -> p (n w)") for part in (group, codes, scales))
+            return group, call
+
+        def transpose_exp(rows, group):
             bank = transpose_words(rows[:].bitcast(F32))
-            e_group = grouped.tile([P, 2 * P * PACK], BF16, bufs=4, align_bytes=64)
-            group_words(bank, e_group[:])
-            bufs = steps_kept + 2
-            codes = packed.tile([P, 2 * P], U32, tag=which + "_codes", bufs=bufs, align_bytes=64)
-            scales = packed.tile([P, 2 * P], U8, tag=which + "_scales", bufs=bufs, align_bytes=64)
-            return codes, scales, (e_group[:], codes[:], scales[:])
+            group_words(bank, group)
 
         def score_rows(b, pair):
             banks = []
@@ -265,10 +282,13 @@ def tile_coattention_pa_t_kernel(tc, q, k, x1, x2, mask, Wv, bv, out_0, out_1):
                     out=row_max[:, first + c : first + c + 1], in_=bank[:], op=ALU.max, axis=AXIS.X
                 )
                 banks.append(bank)
-            nc.vector.tensor_scalar_mul(
+            nc.gpsimd.tensor_scalar(
                 out=row_shift[:, first : first + 2],
                 in0=row_max[:, first : first + 2],
                 scalar1=-SCALE,
+                scalar2=0.0,
+                op0=ALU.mult,
+                op1=ALU.add,
             )
             return banks
 
@@ -287,16 +307,20 @@ def tile_coattention_pa_t_kernel(tc, q, k, x1, x2, mask, Wv, bv, out_0, out_1):
                     accum_out=sums[:, unit, 1 + c : 2 + c],
                 )
 
-        def project(b, block):
-            if block == 0:
+        def project(b, quarter):
+            if quarter == 0:
                 codes = packed.tile([P, 3, D], U32, tag="v_codes", align_bytes=64)
                 scales = packed.tile([P, 3, D], U8, tag="v_scales", align_bytes=64)
                 v_codes[b] = codes
                 v_scales[b] = scales
-            cols = slice(block * P, (block + 1) * P)
-            v_group = grouped.tile([P, 3, P, PACK], BF16, align_bytes=64)
             calls = []
-            for w in range(3):
+            for n in range(3 * quarter, 3 * quarter + 3):
+                w, block = divmod(n, 4)
+                cols = slice(block * P, (block + 1) * P)
+                if block == 0:
+                    v_pass = grouped.tile([P, D, PACK], BF16, align_bytes=64)
+                    v_group[(b, w)] = v_pass
+                group = v_group[(b, w)]
                 bank = psum.tile([P, PACK, P], F32, tag="bank", bufs=6)
                 for t in range(PACK):
                     rows = slice((PACK * w + t) * P, (PACK * w + t + 1) * P)
@@ -310,23 +334,31 @@ def tile_coattention_pa_t_kernel(tc, q, k, x1, x2, mask, Wv, bv, out_0, out_1):
                         stop=True,
                     )
                 nc.vector.tensor_tensor(
-                    out=v_group[:, w, :, :],
+                    out=group[:, cols, :],
                     in0=bank[:].rearrange("p t d -> p d t"),
                     in1=bias[:, cols].unsqueeze(2).to_broadcast([P, P, PACK]),
                     op=ALU.add,
                 )
-                calls.append(
-                    (
-                        v_group[:, w, :, :].rearrange("p d t -> p (d t)"),
-                        v_codes[b][:, w, cols],
-                        v_scales[b][:, w, cols],
+                if block == 3:
+                    calls.append(
+                        (
+                            group[:].rearrange("p d t -> p (d t)"),
+                            v_codes[b][:, w, :],
+                            v_scales[b][:, w, :],
+                        )
                     )
-                )
             return calls
 
         def output_weights(b, quarter):
-            unit = QUARTERS * b + quarter
-            nc.vector.reciprocal(weights[:, unit, :], sums[:, unit, :])
+            if quarter % 2 == 0:
+                pair = slice(QUARTERS * b + quarter, QUARTERS * b + quarter + 2)
+                nc.vector.reciprocal(weights[:, pair, :], sums[:, pair, :])
+                nc.gpsimd.tensor_tensor(
+                    out=mid_weights[:, pair],
+                    in0=weights[:, pair, 0],
+                    in1=keep[:, pair],
+                    op=ALU.mult,
+                )
 
         def x1_mid_rows(b, j):
             unit = QUARTERS * b + j
@@ -343,17 +375,12 @@ def tile_coattention_pa_t_kernel(tc, q, k, x1, x2, mask, Wv, bv, out_0, out_1):
                     stop=(g == 1),
                 )
             mid = results.tile([P, D], F32)
-            nc.vector.tensor_scalar(
-                out=mid[:],
-                in0=bank[:],
-                scalar1=weights[:, unit, 0:1],
-                scalar2=keep[:, unit : unit + 1],
-                op0=ALU.mult,
-                op1=ALU.mult,
+            nc.vector.tensor_scalar_mul(
+                out=mid[:], in0=bank[:], scalar1=mid_weights[:, unit : unit + 1]
             )
             nc.sync.dma_start(out=out_1[b, j * P : (j + 1) * P, :], in_=mid[:])
 
-        def x2_out_rows(b, pair):
+        def x2_out_rows(b, pair, on_vector):
             unit = QUARTERS * b + pair
             both = results.tile([P, 2, D], F32)
             for c in range(2):
@@ -368,12 +395,13 @@ def tile_coattention_pa_t_kernel(tc, q, k, x1, x2, mask, Wv, bv, out_0, out_1):
                     start=True,
                     stop=True,
                 )
-                nc.scalar.activation(
-                    out=both[:, c, :],
-                    in_=bank[:],
-                    func=ACT.Copy,
-                    scale=weights[:, unit, 1 + c : 2 + c],
-                )
+                weight = weights[:, unit, 1 + c : 2 + c]
+                if c >= 2 - on_vector:
+                    nc.vector.tensor_scalar_mul(out=both[:, c, :], in0=bank[:], scalar1=weight)
+                else:
+                    nc.scalar.activation(
+                        out=both[:, c, :], in_=bank[:], func=ACT.Copy, scale=weight
+                    )
             rows = out_0[b, pair * 256 : (pair + 1) * 256, :]
             nc.sync.dma_start(out=rows.rearrange("(c m) d -> m c d", m=P), in_=both[:])
 
@@ -387,47 +415,58 @@ def tile_coattention_pa_t_kernel(tc, q, k, x1, x2, mask, Wv, bv, out_0, out_1):
                 output_weights(*outputs)
 
             e1_unit = unit_of(step, AT_E1)
+            e2_unit = unit_of(step, AT_E2)
+            rows_unit = unit_of(step, AT_ROWS)
+            scores_unit = unit_of(step, AT_SCORES)
+            inputs_unit = unit_of(step, AT_INPUTS)
+            project_unit = unit_of(step, AT_PROJECT)
             if e1_unit:
                 e1_rows = exp_columns(*e1_unit)
 
-            scores_unit = unit_of(step, AT_SCORES)
-            inputs_unit = unit_of(step, AT_INPUTS)
             if inputs_unit:
                 to_quantise.extend(start_input(*inputs_unit))
             for piece in range(PIECES):
                 if scores_unit and piece < 2:
-                    score_bank(scores_unit[0], scores_unit[1], piece)
+                    b, quarter = scores_unit
+                    score_bank(b, 2 * (quarter % 2) + piece, quarter // 2)
                 if inputs_unit:
                     transpose_input(inputs_unit[0], inputs_unit[1], piece)
-            if scores_unit:
-                column_shift(*scores_unit)
+            if scores_unit and scores_unit[1] >= 2:
+                for n in range(2):
+                    column_shift(scores_unit[0], 2 * (scores_unit[1] - 2) + n)
             if inputs_unit and step + LOAD_AHEAD < UNITS:
                 load(step + LOAD_AHEAD)
 
+            banks = score_rows(*rows_unit) if rows_unit else []
             if step == AT_SCORES - 1:
                 transpose_mask()
             if step == AT_PROJECT - 1:
                 to_quantise.append(transpose_wv())
-            rows_unit = unit_of(step, AT_ROWS)
-            if rows_unit:
-                banks = score_rows(*rows_unit)
-            if e1_unit:
-                e1_codes[e1_unit], e1_scales[e1_unit], call = transpose_exp(
-                    e1_rows, "e1", AT_OUTPUTS - AT_E1
-                )
+            group = None
+            if e1_unit or e2_unit:
+                group, call = start_exponentials(e1_unit, e2_unit)
                 to_quantise.append(call)
-            unit = unit_of(step, AT_E2)
-            if unit:
-                e2_codes[unit], e2_scales[unit], call = transpose_exp(
-                    e2_rows[unit], "e2", AT_OUTPUTS - AT_E2
-                )
-                to_quantise.append(call)
-            if rows_unit:
-                exp_rows(rows_unit[0], rows_unit[1], banks)
+            late = step >= UNITS + AT_SCORES
+            if late:
+                if e2_unit:
+                    transpose_exp(e2_rows[e2_unit], group[:, 1 if e1_unit else 0, :])
+                if outputs:
+                    x1_mid_rows(*outputs)
+                    x2_out_rows(*outputs, 1 + (step > UNITS + AT_SCORES))
+                if rows_unit:
+                    exp_rows(rows_unit[0], rows_unit[1], banks)
+                if e1_unit:
+                    transpose_exp(e1_rows, group[:, 0, :])
+            else:
+                if e1_unit:
+                    transpose_exp(e1_rows, group[:, 0, :])
+                if e2_unit:
+                    transpose_exp(e2_rows[e2_unit], group[:, 1 if e1_unit else 0, :])
+                if rows_unit:
+                    exp_rows(rows_unit[0], rows_unit[1], banks)
 
-            unit = unit_of(step, AT_PROJECT)
-            if unit:
-                to_quantise.extend(project(*unit))
-            if outputs:
+            if project_unit:
+                to_quantise.extend(project(*project_unit))
+            if outputs and not late:
                 x1_mid_rows(*outputs)
-                x2_out_rows(*outputs)
+                x2_out_rows(*outputs, 0)

@@ -25,14 +25,16 @@ MASKED = 2.0**104
 QUARTERS = 4
 UNITS = QUARTERS * B
 AT_INPUTS = 0
-AT_SCORES = 2
-AT_E1 = 5
+AT_SCORES = 1
+AT_E1 = 4
 AT_PROJECT = 3
-AT_ROWS = 4
-AT_E2 = 5
+AT_ROWS = 3
+AT_E2 = 4
 AT_OUTPUTS = 7
 STEPS = UNITS + AT_OUTPUTS
 PIECES = 3
+PIECE_ORDER = (2, 0, 1)
+WARM_UP = 5
 LOAD_AHEAD = 8
 
 
@@ -85,7 +87,7 @@ def tile_coattention_pa_t_kernel(tc, q, k, x1, x2, mask, Wv, bv, out_0, out_1):
         def load(n):
             b, quarter = divmod(n, QUARTERS)
             half = quarter % 2
-            for piece in range(PIECES):
+            for piece in PIECE_ORDER:
                 long_one, short_one = (q, k) if quarter < 2 else (x1, x2)
                 source = long_one if piece < 2 else short_one
                 first = (2 * half + piece) * 256 if piece < 2 else half * 256
@@ -97,13 +99,19 @@ def tile_coattention_pa_t_kernel(tc, q, k, x1, x2, mask, Wv, bv, out_0, out_1):
                     nc.sync.dma_start(out=tile_in[:], in_=rows.rearrange("(m e) d -> m e d", e=2))
                 loaded[(n, piece)] = tile_in
 
+        zeros = const.tile([P, BANK], BF16)
+        nc.vector.memset(zeros[:], 0.0)
+        for n in range(WARM_UP):
+            bank = psum.tile([P, BANK], F32, tag="bank", bufs=6)
+            nc.tensor.matmul(bank[:], lhsT=zeros[:, 0:P], rhs=zeros[:], start=True, stop=True)
+
         load(0)
-        load(1)
         mask_rows = const.tile([P, P], BF16)
         nc.vector.memset(mask_rows[:], 0.0)
         nc.sync.dma_start(
             out=mask_rows[0:UNITS, :], in_=mask.rearrange("b (j p) -> (b j) p", p=P)
         )
+        load(1)
         wv_rows = const.tile([P, 4, D], BF16)
         nc.sync.dma_start(out=wv_rows[:], in_=Wv.rearrange("(c m) d -> m c d", m=P))
         load(2)
@@ -375,9 +383,11 @@ def tile_coattention_pa_t_kernel(tc, q, k, x1, x2, mask, Wv, bv, out_0, out_1):
                     stop=(g == 1),
                 )
             mid = results.tile([P, D], F32)
-            nc.vector.tensor_scalar_mul(
-                out=mid[:], in0=bank[:], scalar1=mid_weights[:, unit : unit + 1]
-            )
+            weight = mid_weights[:, unit : unit + 1]
+            if j == QUARTERS - 1:
+                nc.scalar.activation(out=mid[:], in_=bank[:], func=ACT.Copy, scale=weight)
+            else:
+                nc.vector.tensor_scalar_mul(out=mid[:], in0=bank[:], scalar1=weight)
             nc.sync.dma_start(out=out_1[b, j * P : (j + 1) * P, :], in_=mid[:])
 
         def x2_out_rows(b, pair, on_vector):
@@ -402,8 +412,12 @@ def tile_coattention_pa_t_kernel(tc, q, k, x1, x2, mask, Wv, bv, out_0, out_1):
                     nc.scalar.activation(
                         out=both[:, c, :], in_=bank[:], func=ACT.Copy, scale=weight
                     )
-            rows = out_0[b, pair * 256 : (pair + 1) * 256, :]
-            nc.sync.dma_start(out=rows.rearrange("(c m) d -> m c d", m=P), in_=both[:])
+            rows = out_0[b, pair * 256 : (pair + 1) * 256, :].rearrange("(c m) d -> m c d", m=P)
+            if b == B - 1 and pair == QUARTERS - 1:
+                for c in range(2):
+                    nc.sync.dma_start(out=rows[:, c, :], in_=both[:, c, :])
+            else:
+                nc.sync.dma_start(out=rows, in_=both[:])
 
         to_quantise = []
         for step in range(STEPS):
@@ -425,12 +439,20 @@ def tile_coattention_pa_t_kernel(tc, q, k, x1, x2, mask, Wv, bv, out_0, out_1):
 
             if inputs_unit:
                 to_quantise.extend(start_input(*inputs_unit))
-            for piece in range(PIECES):
-                if scores_unit and piece < 2:
-                    b, quarter = scores_unit
-                    score_bank(b, 2 * (quarter % 2) + piece, quarter // 2)
-                if inputs_unit:
-                    transpose_input(inputs_unit[0], inputs_unit[1], piece)
+            if step == AT_SCORES:
+                transpose_mask()
+            score_work = []
+            if scores_unit:
+                b, quarter = scores_unit
+                score_work = [(b, 2 * (quarter % 2) + n, quarter // 2) for n in range(2)]
+            input_work = [(inputs_unit[0], inputs_unit[1], n) for n in PIECE_ORDER if inputs_unit]
+            for n in range(PIECES):
+                if step == AT_SCORES and n < len(input_work):
+                    transpose_input(*input_work[n])
+                if n < len(score_work):
+                    score_bank(*score_work[n])
+                if step != AT_SCORES and n < len(input_work):
+                    transpose_input(*input_work[n])
             if scores_unit and scores_unit[1] >= 2:
                 for n in range(2):
                     column_shift(scores_unit[0], 2 * (scores_unit[1] - 2) + n)
@@ -438,8 +460,6 @@ def tile_coattention_pa_t_kernel(tc, q, k, x1, x2, mask, Wv, bv, out_0, out_1):
                 load(step + LOAD_AHEAD)
 
             banks = score_rows(*rows_unit) if rows_unit else []
-            if step == AT_SCORES - 1:
-                transpose_mask()
             if step == AT_PROJECT - 1:
                 to_quantise.append(transpose_wv())
             group = None
@@ -452,7 +472,7 @@ def tile_coattention_pa_t_kernel(tc, q, k, x1, x2, mask, Wv, bv, out_0, out_1):
                     transpose_exp(e2_rows[e2_unit], group[:, 1 if e1_unit else 0, :])
                 if outputs:
                     x1_mid_rows(*outputs)
-                    x2_out_rows(*outputs, 1 + (step > UNITS + AT_SCORES))
+                    x2_out_rows(*outputs, 1)
                 if rows_unit:
                     exp_rows(rows_unit[0], rows_unit[1], banks)
                 if e1_unit:

@@ -48,13 +48,14 @@ def tile_coattention_pa_t_kernel(tc, q, k, x1, x2, mask, Wv, bv, out_0, out_1):
         packed = ctx.enter_context(tc.tile_pool(name="packed", bufs=2))
         scores = ctx.enter_context(tc.tile_pool(name="scores", bufs=8))
         exps = ctx.enter_context(tc.tile_pool(name="exps", bufs=3))
-        results = ctx.enter_context(tc.tile_pool(name="results", bufs=3))
+        results = ctx.enter_context(tc.tile_pool(name="results", bufs=5))
         psum = ctx.enter_context(tc.psum_pool(name="psum", bufs=8))
         ctx.enter_context(tc.manual_schedule())
 
         def transpose_words(words):
-            bank = psum.tile([P, 2, 2, P], F32, tag="bank", bufs=6)
-            for block in range(2):
+            blocks = words.shape[1]
+            bank = psum.tile([P, blocks, 2, P], F32, tag="bank", bufs=6)
+            for block in range(blocks):
                 for u in range(2):
                     nc.tensor.transpose(
                         bank[:, block, u, :], words[:, block, u * P : (u + 1) * P], ident[:]
@@ -87,13 +88,16 @@ def tile_coattention_pa_t_kernel(tc, q, k, x1, x2, mask, Wv, bv, out_0, out_1):
         def load(n):
             b, quarter = divmod(n, QUARTERS)
             half = quarter % 2
-            for piece in PIECE_ORDER:
+            for piece in (0, 1, 2) if n == 0 else PIECE_ORDER:
                 long_one, short_one = (q, k) if quarter < 2 else (x1, x2)
                 source = long_one if piece < 2 else short_one
                 first = (2 * half + piece) * 256 if piece < 2 else half * 256
                 rows = source[b, first : first + 256, :]
                 tile_in = inputs.tile([P, 2, D], BF16)
-                if quarter < 2:
+                if n == 0 and piece == 2:
+                    for c in range(2):
+                        nc.sync.dma_start(out=tile_in[:, c, :], in_=rows[c * P : (c + 1) * P, :])
+                elif quarter < 2:
                     nc.sync.dma_start(out=tile_in[:], in_=rows.rearrange("(c m) d -> m c d", m=P))
                 else:
                     nc.sync.dma_start(out=tile_in[:], in_=rows.rearrange("(m e) d -> m e d", e=2))
@@ -183,17 +187,19 @@ def tile_coattention_pa_t_kernel(tc, q, k, x1, x2, mask, Wv, bv, out_0, out_1):
                 (group[:, 2048:3072], x_codes[b][:, x2_cols], x_scales[b][:, x2_cols]),
             ]
 
-        def transpose_input(b, quarter, piece):
+        def transpose_input(b, quarter, piece, blocks=slice(0, 2)):
             half = quarter % 2
-            bank = transpose_words(loaded[(QUARTERS * b + quarter, piece)][:].bitcast(F32))
+            words = loaded[(QUARTERS * b + quarter, piece)][:].bitcast(F32)
+            bank = transpose_words(words[:, blocks, :])
             if quarter < 2:
                 if piece < 2:
                     first = (2 * half + piece) * 256
                     target = q_turned[b][:, :, first : first + 256]
                 else:
                     target = k_turned[b][:, :, half * 256 : (half + 1) * 256]
+                target = target.rearrange("p u (c r) -> p u c r", c=2)
                 nc.scalar.copy(
-                    out=target.rearrange("p u (c r) -> p u c r", c=2),
+                    out=target[:, :, blocks, :],
                     in_=bank[:].rearrange("p c u r -> p u c r"),
                 )
             else:
@@ -290,14 +296,14 @@ def tile_coattention_pa_t_kernel(tc, q, k, x1, x2, mask, Wv, bv, out_0, out_1):
                     out=row_max[:, first + c : first + c + 1], in_=bank[:], op=ALU.max, axis=AXIS.X
                 )
                 banks.append(bank)
-            nc.gpsimd.tensor_scalar(
-                out=row_shift[:, first : first + 2],
-                in0=row_max[:, first : first + 2],
-                scalar1=-SCALE,
-                scalar2=0.0,
-                op0=ALU.mult,
-                op1=ALU.add,
-            )
+                nc.gpsimd.tensor_scalar(
+                    out=row_shift[:, first + c : first + c + 1],
+                    in0=row_max[:, first + c : first + c + 1],
+                    scalar1=-SCALE,
+                    scalar2=0.0,
+                    op0=ALU.mult,
+                    op1=ALU.add,
+                )
             return banks
 
         def exp_rows(b, pair, banks):
@@ -384,7 +390,7 @@ def tile_coattention_pa_t_kernel(tc, q, k, x1, x2, mask, Wv, bv, out_0, out_1):
                 )
             mid = results.tile([P, D], F32)
             weight = mid_weights[:, unit : unit + 1]
-            if j == QUARTERS - 1:
+            if j % 2 == 1:
                 nc.scalar.activation(out=mid[:], in_=bank[:], func=ACT.Copy, scale=weight)
             else:
                 nc.vector.tensor_scalar_mul(out=mid[:], in0=bank[:], scalar1=weight)
@@ -446,7 +452,9 @@ def tile_coattention_pa_t_kernel(tc, q, k, x1, x2, mask, Wv, bv, out_0, out_1):
                 b, quarter = scores_unit
                 score_work = [(b, 2 * (quarter % 2) + n, quarter // 2) for n in range(2)]
             input_work = [(inputs_unit[0], inputs_unit[1], n) for n in PIECE_ORDER if inputs_unit]
-            for n in range(PIECES):
+            if step == 0:
+                input_work = [(0, 0, 0), (0, 0, 1), (0, 0, 2, slice(0, 1)), (0, 0, 2, slice(1, 2))]
+            for n in range(max(PIECES, len(input_work))):
                 if step == AT_SCORES and n < len(input_work):
                     transpose_input(*input_work[n])
                 if n < len(score_work):

@@ -35,7 +35,7 @@ STEPS = UNITS + AT_OUTPUTS
 PIECES = 3
 PIECE_ORDER = (2, 0, 1)
 WARM_UP = 5
-LOAD_AHEAD = 8
+LOAD_AHEAD = 5
 
 
 def tile_coattention_pa_t_kernel(tc, q, k, x1, x2, mask, Wv, bv, out_0, out_1):
@@ -44,10 +44,10 @@ def tile_coattention_pa_t_kernel(tc, q, k, x1, x2, mask, Wv, bv, out_0, out_1):
         const = ctx.enter_context(tc.tile_pool(name="const", bufs=1))
         inputs = ctx.enter_context(tc.tile_pool(name="inputs", bufs=PIECES * LOAD_AHEAD))
         turned = ctx.enter_context(tc.tile_pool(name="turned", bufs=2))
-        grouped = ctx.enter_context(tc.tile_pool(name="grouped", bufs=2))
+        grouped = ctx.enter_context(tc.tile_pool(name="grouped", bufs=3))
         packed = ctx.enter_context(tc.tile_pool(name="packed", bufs=2))
         scores = ctx.enter_context(tc.tile_pool(name="scores", bufs=8))
-        exps = ctx.enter_context(tc.tile_pool(name="exps", bufs=3))
+        exps = ctx.enter_context(tc.tile_pool(name="exps", bufs=4))
         results = ctx.enter_context(tc.tile_pool(name="results", bufs=5))
         psum = ctx.enter_context(tc.psum_pool(name="psum", bufs=8))
         ctx.enter_context(tc.manual_schedule())
@@ -143,9 +143,9 @@ def tile_coattention_pa_t_kernel(tc, q, k, x1, x2, mask, Wv, bv, out_0, out_1):
                 op1=ALU.mult,
             )
 
-        wv_group = const.tile([P, D * PACK], BF16, align_bytes=64)
-        wv_codes = const.tile([P, D], U32, align_bytes=64)
-        wv_scales = const.tile([P, D], U8, align_bytes=64)
+        wv_group = const.tile([P, D * PACK], BF16, align_bytes=256)
+        wv_codes = const.tile([P, D], U32, align_bytes=256)
+        wv_scales = const.tile([P, D], U8, align_bytes=256)
 
         def transpose_wv():
             words = wv_rows[:].bitcast(F32)
@@ -172,13 +172,13 @@ def tile_coattention_pa_t_kernel(tc, q, k, x1, x2, mask, Wv, bv, out_0, out_1):
                 q_turned[b] = q_words
                 k_turned[b] = k_words
             if quarter == 2:
-                codes = packed.tile([P, 12 * P], U32, tag="x_codes", align_bytes=64)
-                scales = packed.tile([P, 12 * P], U8, tag="x_scales", align_bytes=64)
+                codes = packed.tile([P, 12 * P], U32, tag="x_codes", align_bytes=256)
+                scales = packed.tile([P, 12 * P], U8, tag="x_scales", align_bytes=256)
                 x_codes[b] = codes
                 x_scales[b] = scales
             if quarter < 2:
                 return []
-            group = grouped.tile([P, PIECES * 2 * P * PACK], BF16, tag="x_group", align_bytes=64)
+            group = grouped.tile([P, PIECES * 2 * P * PACK], BF16, tag="x_group", align_bytes=256)
             x_group[b] = group
             x1_cols = slice(half * 512, (half + 1) * 512)
             x2_cols = slice(1024 + half * 256, 1024 + (half + 1) * 256)
@@ -262,13 +262,13 @@ def tile_coattention_pa_t_kernel(tc, q, k, x1, x2, mask, Wv, bv, out_0, out_1):
             count = len(units)
             bufs = AT_OUTPUTS - AT_E1 + 2
             group = grouped.tile(
-                [P, count, 2 * P * PACK], BF16, tag="e_group%d" % count, align_bytes=64
+                [P, count, 2 * P * PACK], BF16, tag="e_group%d" % count, align_bytes=256
             )
             codes = packed.tile(
-                [P, count, 2 * P], U32, tag="e_codes%d" % count, bufs=bufs, align_bytes=64
+                [P, count, 2 * P], U32, tag="e_codes%d" % count, bufs=bufs, align_bytes=256
             )
             scales = packed.tile(
-                [P, count, 2 * P], U8, tag="e_scales%d" % count, bufs=bufs, align_bytes=64
+                [P, count, 2 * P], U8, tag="e_scales%d" % count, bufs=bufs, align_bytes=256
             )
             for n, (all_codes, all_scales, unit) in enumerate(units):
                 all_codes[unit] = codes[:, n, :]
@@ -323,8 +323,8 @@ def tile_coattention_pa_t_kernel(tc, q, k, x1, x2, mask, Wv, bv, out_0, out_1):
 
         def project(b, quarter):
             if quarter == 0:
-                codes = packed.tile([P, 3, D], U32, tag="v_codes", align_bytes=64)
-                scales = packed.tile([P, 3, D], U8, tag="v_scales", align_bytes=64)
+                codes = packed.tile([P, 3, D], U32, tag="v_codes", align_bytes=256)
+                scales = packed.tile([P, 3, D], U8, tag="v_scales", align_bytes=256)
                 v_codes[b] = codes
                 v_scales[b] = scales
             calls = []
@@ -332,7 +332,7 @@ def tile_coattention_pa_t_kernel(tc, q, k, x1, x2, mask, Wv, bv, out_0, out_1):
                 w, block = divmod(n, 4)
                 cols = slice(block * P, (block + 1) * P)
                 if block == 0:
-                    v_pass = grouped.tile([P, D, PACK], BF16, align_bytes=64)
+                    v_pass = grouped.tile([P, D, PACK], BF16, align_bytes=256)
                     v_group[(b, w)] = v_pass
                 group = v_group[(b, w)]
                 bank = psum.tile([P, PACK, P], F32, tag="bank", bufs=6)
@@ -390,7 +390,7 @@ def tile_coattention_pa_t_kernel(tc, q, k, x1, x2, mask, Wv, bv, out_0, out_1):
                 )
             mid = results.tile([P, D], F32)
             weight = mid_weights[:, unit : unit + 1]
-            if j % 2 == 1:
+            if j == 3:
                 nc.scalar.activation(out=mid[:], in_=bank[:], func=ACT.Copy, scale=weight)
             else:
                 nc.vector.tensor_scalar_mul(out=mid[:], in0=bank[:], scalar1=weight)
@@ -431,8 +431,9 @@ def tile_coattention_pa_t_kernel(tc, q, k, x1, x2, mask, Wv, bv, out_0, out_1):
                 nc.vector.quantize_mx(out=codes.bitcast(FP8X4), scales=scales, in_=group)
             to_quantise = []
             outputs = unit_of(step, AT_OUTPUTS)
-            if outputs:
-                output_weights(*outputs)
+            next_outputs = unit_of(step + 1, AT_OUTPUTS)
+            if next_outputs:
+                output_weights(*next_outputs)
 
             e1_unit = unit_of(step, AT_E1)
             e2_unit = unit_of(step, AT_E2)

import math
from contextlib import ExitStack

import concourse.mybir as mybir
from concourse.masks import make_identity

F32 = mybir.dt.float32
BF16 = mybir.dt.bfloat16
U32 = mybir.dt.uint32
U8 = mybir.dt.uint8
FP8X4 = mybir.dt.float8_e4m3fn_x4
ALU = mybir.AluOpType
ACT = mybir.ActivationFunctionType
AXIS = mybir.AxisListType

B, L1, L2, D = 4, 1024, 512, 512
P = 128
PACK = 4
BANK = 512
FLOPS = 2 * B * (L1 * D * D + L2 * D * D + 3 * L1 * L2 * D)

SCALE = 1.0 / math.sqrt(D)
MASKED = 2.0**104

QUARTERS = 4
UNITS = QUARTERS * B
AT_INPUTS = 0
AT_SCORES = 1
AT_E1 = 4
AT_PROJECT = 3
AT_ROWS = 3
AT_E2 = 4
AT_OUTPUTS = 7
STEPS = UNITS + AT_OUTPUTS
PIECES = 3
PIECE_ORDER = (2, 0, 1)
WARM_UP = 5
LOAD_AHEAD = 5


def tile_coattention_pa_t_kernel(tc, q, k, x1, x2, mask, Wv, bv, out_0, out_1):
    nc = tc.nc
    with ExitStack() as ctx:
        const = ctx.enter_context(tc.tile_pool(name="const", bufs=1))
        inputs = ctx.enter_context(tc.tile_pool(name="inputs", bufs=PIECES * LOAD_AHEAD))
        turned = ctx.enter_context(tc.tile_pool(name="turned", bufs=2))
        grouped = ctx.enter_context(tc.tile_pool(name="grouped", bufs=3))
        packed = ctx.enter_context(tc.tile_pool(name="packed", bufs=2))
        scores = ctx.enter_context(tc.tile_pool(name="scores", bufs=8))
        exps = ctx.enter_context(tc.tile_pool(name="exps", bufs=4))
        results = ctx.enter_context(tc.tile_pool(name="results", bufs=5))
        psum = ctx.enter_context(tc.psum_pool(name="psum", bufs=8))
        ctx.enter_context(tc.manual_schedule())

        def transpose_words(words):
            blocks = words.shape[1]
            bank = psum.tile([P, blocks, 2, P], F32, tag="bank", bufs=6)
            for block in range(blocks):
                for u in range(2):
                    nc.tensor.transpose(
                        bank[:, block, u, :], words[:, block, u * P : (u + 1) * P], ident[:]
                    )
            return bank

        def group_words(bank, group):
            nc.scalar.copy(
                out=group.bitcast(F32).rearrange("p (c r u) -> p c r u", c=2, u=2),
                in_=bank[:].rearrange("p c u r -> p c r u"),
            )

        def unit_of(step, offset):
            n = step - offset
            return divmod(n, QUARTERS) if 0 <= n < UNITS else None

        ident = const.tile([P, P], F32)
        make_identity(nc, ident[:])

        col_max = const.tile([P, 2 * UNITS], F32)
        col_shift = const.tile([P, UNITS], F32)
        row_max = const.tile([P, 2 * UNITS], F32)
        row_shift = const.tile([P, 2 * UNITS], F32)
        sums = const.tile([P, UNITS, 3], F32)
        weights = const.tile([P, UNITS, 3], F32)
        mid_weights = const.tile([P, UNITS], F32)

        loaded = {}

        def load(n):
            b, quarter = divmod(n, QUARTERS)
            half = quarter % 2
            for piece in (0, 1, 2) if n == 0 else PIECE_ORDER:
                long_one, short_one = (q, k) if quarter < 2 else (x1, x2)
                source = long_one if piece < 2 else short_one
                first = (2 * half + piece) * 256 if piece < 2 else half * 256
                rows = source[b, first : first + 256, :]
                tile_in = inputs.tile([P, 2, D], BF16)
                if n == 0 and piece == 2:
                    for c in range(2):
                        nc.sync.dma_start(out=tile_in[:, c, :], in_=rows[c * P : (c + 1) * P, :])
                elif quarter < 2:
                    nc.sync.dma_start(out=tile_in[:], in_=rows.rearrange("(c m) d -> m c d", m=P))
                else:
                    nc.sync.dma_start(out=tile_in[:], in_=rows.rearrange("(m e) d -> m e d", e=2))
                loaded[(n, piece)] = tile_in

        zeros = const.tile([P, BANK], BF16)
        nc.vector.memset(zeros[:], 0.0)
        for n in range(WARM_UP):
            bank = psum.tile([P, BANK], F32, tag="bank", bufs=6)
            nc.tensor.matmul(bank[:], lhsT=zeros[:, 0:P], rhs=zeros[:], start=True, stop=True)

        load(0)
        mask_rows = const.tile([P, P], BF16)
        nc.vector.memset(mask_rows[:], 0.0)
        nc.sync.dma_start(
            out=mask_rows[0:UNITS, :], in_=mask.rearrange("b (j p) -> (b j) p", p=P)
        )
        load(1)
        wv_rows = const.tile([P, 4, D], BF16)
        nc.sync.dma_start(out=wv_rows[:], in_=Wv.rearrange("(c m) d -> m c d", m=P))
        load(2)
        load(3)
        bias = const.tile([P, D], BF16)
        nc.sync.dma_start(out=bias[:], in_=bv.partition_broadcast(P))
        for n in range(4, LOAD_AHEAD):
            load(n)

        keep = const.tile([P, UNITS], F32)
        mask_term = const.tile([P, UNITS], F32)

        def transpose_mask():
            mask_f32 = const.tile([P, P], F32)
            nc.vector.tensor_copy(out=mask_f32[:], in_=mask_rows[:])
            mask_bank = psum.tile([P, P], F32, tag="bank", bufs=6)
            nc.tensor.transpose(mask_bank[:], mask_f32[:], ident[:])
            nc.vector.tensor_copy(out=keep[:], in_=mask_bank[:, 0:UNITS])
            nc.vector.tensor_scalar(
                out=mask_term[:],
                in0=keep[:],
                scalar1=-1.0,
                scalar2=MASKED,
                op0=ALU.add,
                op1=ALU.mult,
            )

        wv_group = const.tile([P, D * PACK], BF16, align_bytes=256)
        wv_codes = const.tile([P, D], U32, align_bytes=256)
        wv_scales = const.tile([P, D], U8, align_bytes=256)

        def transpose_wv():
            words = wv_rows[:].bitcast(F32)
            for pair in range(2):
                bank = transpose_words(words[:, 2 * pair : 2 * pair + 2, :])
                group_words(bank, wv_group[:, pair * 1024 : (pair + 1) * 1024])
            return (wv_group[:], wv_codes[:], wv_scales[:])

        q_turned, k_turned = {}, {}
        x_group = {}
        x_codes, x_scales = {}, {}
        v_codes, v_scales = {}, {}
        v_group = {}
        a_turned = {}
        e1_codes, e1_scales = {}, {}
        e2_rows = {}
        e2_codes, e2_scales = {}, {}

        def start_input(b, quarter):
            half = quarter % 2
            if quarter == 0:
                q_words = turned.tile([P, 2, L1], F32)
                k_words = turned.tile([P, 2, L2], F32)
                q_turned[b] = q_words
                k_turned[b] = k_words
            if quarter == 2:
                codes = packed.tile([P, 12 * P], U32, tag="x_codes", align_bytes=256)
                scales = packed.tile([P, 12 * P], U8, tag="x_scales", align_bytes=256)
                x_codes[b] = codes
                x_scales[b] = scales
            if quarter < 2:
                return []
            group = grouped.tile([P, PIECES * 2 * P * PACK], BF16, tag="x_group", align_bytes=256)
            x_group[b] = group
            x1_cols = slice(half * 512, (half + 1) * 512)
            x2_cols = slice(1024 + half * 256, 1024 + (half + 1) * 256)
            return [
                (group[:, 0:2048], x_codes[b][:, x1_cols], x_scales[b][:, x1_cols]),
                (group[:, 2048:3072], x_codes[b][:, x2_cols], x_scales[b][:, x2_cols]),
            ]

        def transpose_input(b, quarter, piece, blocks=slice(0, 2)):
            half = quarter % 2
            words = loaded[(QUARTERS * b + quarter, piece)][:].bitcast(F32)
            bank = transpose_words(words[:, blocks, :])
            if quarter < 2:
                if piece < 2:
                    first = (2 * half + piece) * 256
                    target = q_turned[b][:, :, first : first + 256]
                else:
                    target = k_turned[b][:, :, half * 256 : (half + 1) * 256]
                target = target.rearrange("p u (c r) -> p u c r", c=2)
                nc.scalar.copy(
                    out=target[:, :, blocks, :],
                    in_=bank[:].rearrange("p c u r -> p u c r"),
                )
            else:
                group_words(bank, x_group[b][:, piece * 1024 : (piece + 1) * 1024])

        def score_bank(b, j, h):
            q_el = q_turned[b][:].bitcast(BF16).rearrange("p u (l e) -> p u l e", e=2)
            k_el = k_turned[b][:].bitcast(BF16).rearrange("p u (l e) -> p u l e", e=2)
            unit = QUARTERS * b + j
            if h == 0:
                a_rows = scores.tile([P, L1], F32)
                a_turned[(b, j)] = a_rows
            bank = psum.tile([P, BANK], F32, tag="bank", bufs=6)
            for t in range(PACK):
                u, e = divmod(t, 2)
                nc.tensor.matmul(
                    bank[:],
                    lhsT=k_el[:, u, j * P : (j + 1) * P, e],
                    rhs=q_el[:, u, h * BANK : (h + 1) * BANK, e],
                    start=(t == 0),
                    stop=(t == PACK - 1),
                )
            nc.vector.tensor_scalar(
                out=a_turned[(b, j)][:, h * BANK : (h + 1) * BANK],
                in0=bank[:],
                scalar1=mask_term[:, unit : unit + 1],
                scalar2=None,
                op0=ALU.add,
                op1=ALU.max,
                accum_out=col_max[:, 2 * unit + h : 2 * unit + h + 1],
            )

        def column_shift(b, j):
            unit = QUARTERS * b + j
            nc.gpsimd.tensor_scalar(
                out=col_shift[:, unit : unit + 1],
                in0=col_max[:, 2 * unit : 2 * unit + 1],
                scalar1=col_max[:, 2 * unit + 1 : 2 * unit + 2],
                scalar2=-SCALE,
                op0=ALU.max,
                op1=ALU.mult,
            )

        def exp_columns(b, j):
            unit = QUARTERS * b + j
            e1_rows = exps.tile([P, 2, 512], BF16)
            nc.scalar.activation(
                out=e1_rows[:].rearrange("p g l -> p (g l)"),
                in_=a_turned[(b, j)][:],
                func=ACT.Exp,
                bias=col_shift[:, unit : unit + 1],
                scale=SCALE,
                accum_out=sums[:, unit, 0:1],
            )
            return e1_rows

        def start_exponentials(e1_unit, e2_unit):
            units = [(e1_codes, e1_scales, e1_unit), (e2_codes, e2_scales, e2_unit)]
            units = [entry for entry in units if entry[2]]
            count = len(units)
            bufs = AT_OUTPUTS - AT_E1 + 2
            group = grouped.tile(
                [P, count, 2 * P * PACK], BF16, tag="e_group%d" % count, align_bytes=256
            )
            codes = packed.tile(
                [P, count, 2 * P], U32, tag="e_codes%d" % count, bufs=bufs, align_bytes=256
            )
            scales = packed.tile(
                [P, count, 2 * P], U8, tag="e_scales%d" % count, bufs=bufs, align_bytes=256
            )
            for n, (all_codes, all_scales, unit) in enumerate(units):
                all_codes[unit] = codes[:, n, :]
                all_scales[unit] = scales[:, n, :]
            call = tuple(part[:].rearrange("p n w -> p (n w)") for part in (group, codes, scales))
            return group, call

        def transpose_exp(rows, group):
            bank = transpose_words(rows[:].bitcast(F32))
            group_words(bank, group)

        def score_rows(b, pair):
            banks = []
            first = 2 * (QUARTERS * b + pair)
            for c in range(2):
                i = 2 * pair + c
                bank = psum.tile([P, L2], F32, tag="rows", bufs=2)
                for j in range(4):
                    nc.tensor.transpose(
                        bank[:, j * P : (j + 1) * P],
                        a_turned[(b, j)][:, i * P : (i + 1) * P],
                        ident[:],
                    )
                nc.vector.tensor_reduce(
                    out=row_max[:, first + c : first + c + 1], in_=bank[:], op=ALU.max, axis=AXIS.X
                )
                banks.append(bank)
                nc.gpsimd.tensor_scalar(
                    out=row_shift[:, first + c : first + c + 1],
                    in0=row_max[:, first + c : first + c + 1],
                    scalar1=-SCALE,
                    scalar2=0.0,
                    op0=ALU.mult,
                    op1=ALU.add,
                )
            return banks

        def exp_rows(b, pair, banks):
            unit = QUARTERS * b + pair
            first = 2 * unit
            e2_pair = exps.tile([P, 2, L2], BF16)
            e2_rows[(b, pair)] = e2_pair
            for c in range(2):
                nc.scalar.activation(
                    out=e2_pair[:, c, :],
                    in_=banks[c][:],
                    func=ACT.Exp,
                    bias=row_shift[:, first + c : first + c + 1],
                    scale=SCALE,
                    accum_out=sums[:, unit, 1 + c : 2 + c],
                )

        def project(b, quarter):
            if quarter == 0:
                codes = packed.tile([P, 3, D], U32, tag="v_codes", align_bytes=256)
                scales = packed.tile([P, 3, D], U8, tag="v_scales", align_bytes=256)
                v_codes[b] = codes
                v_scales[b] = scales
            calls = []
            for n in range(3 * quarter, 3 * quarter + 3):
                w, block = divmod(n, 4)
                cols = slice(block * P, (block + 1) * P)
                if block == 0:
                    v_pass = grouped.tile([P, D, PACK], BF16, align_bytes=256)
                    v_group[(b, w)] = v_pass
                group = v_group[(b, w)]
                bank = psum.tile([P, PACK, P], F32, tag="bank", bufs=6)
                for t in range(PACK):
                    rows = slice((PACK * w + t) * P, (PACK * w + t + 1) * P)
                    nc.tensor.matmul_mx(
                        out=bank[:, t, :],
                        lhsT=x_codes[b][:, rows].bitcast(FP8X4),
                        lhsT_scale=x_scales[b][:, rows],
                        rhs=wv_codes[:, cols].bitcast(FP8X4),
                        rhs_scale=wv_scales[:, cols],
                        start=True,
                        stop=True,
                    )
                nc.vector.tensor_tensor(
                    out=group[:, cols, :],
                    in0=bank[:].rearrange("p t d -> p d t"),
                    in1=bias[:, cols].unsqueeze(2).to_broadcast([P, P, PACK]),
                    op=ALU.add,
                )
                if block == 3:
                    calls.append(
                        (
                            group[:].rearrange("p d t -> p (d t)"),
                            v_codes[b][:, w, :],
                            v_scales[b][:, w, :],
                        )
                    )
            return calls

        def output_weights(b, quarter):
            if quarter % 2 == 0:
                pair = slice(QUARTERS * b + quarter, QUARTERS * b + quarter + 2)
                nc.vector.reciprocal(weights[:, pair, :], sums[:, pair, :])
                nc.gpsimd.tensor_tensor(
                    out=mid_weights[:, pair],
                    in0=weights[:, pair, 0],
                    in1=keep[:, pair],
                    op=ALU.mult,
                )

        def x1_mid_rows(b, j):
            unit = QUARTERS * b + j
            bank = psum.tile([P, D], F32, tag="bank", bufs=6)
            for g in range(2):
                cols = slice(g * P, (g + 1) * P)
                nc.tensor.matmul_mx(
                    out=bank[:],
                    lhsT=e1_codes[(b, j)][:, cols].bitcast(FP8X4),
                    lhsT_scale=e1_scales[(b, j)][:, cols],
                    rhs=v_codes[b][:, g, :].bitcast(FP8X4),
                    rhs_scale=v_scales[b][:, g, :],
                    start=(g == 0),
                    stop=(g == 1),
                )
            mid = results.tile([P, D], F32)
            weight = mid_weights[:, unit : unit + 1]
            if j == 3:
                nc.scalar.activation(out=mid[:], in_=bank[:], func=ACT.Copy, scale=weight)
            else:
                nc.vector.tensor_scalar_mul(out=mid[:], in0=bank[:], scalar1=weight)
            nc.sync.dma_start(out=out_1[b, j * P : (j + 1) * P, :], in_=mid[:])

        def x2_out_rows(b, pair, on_vector):
            unit = QUARTERS * b + pair
            both = results.tile([P, 2, D], F32)
            for c in range(2):
                cols = slice(c * P, (c + 1) * P)
                bank = psum.tile([P, D], F32, tag="bank", bufs=6)
                nc.tensor.matmul_mx(
                    out=bank[:],
                    lhsT=e2_codes[(b, pair)][:, cols].bitcast(FP8X4),
                    lhsT_scale=e2_scales[(b, pair)][:, cols],
                    rhs=v_codes[b][:, 2, :].bitcast(FP8X4),
                    rhs_scale=v_scales[b][:, 2, :],
                    start=True,
                    stop=True,
                )
                weight = weights[:, unit, 1 + c : 2 + c]
                if c >= 2 - on_vector:
                    nc.vector.tensor_scalar_mul(out=both[:, c, :], in0=bank[:], scalar1=weight)
                else:
                    nc.scalar.activation(
                        out=both[:, c, :], in_=bank[:], func=ACT.Copy, scale=weight
                    )
            rows = out_0[b, pair * 256 : (pair + 1) * 256, :].rearrange("(c m) d -> m c d", m=P)
            if b == B - 1 and pair == QUARTERS - 1:
                for c in range(2):
                    nc.sync.dma_start(out=rows[:, c, :], in_=both[:, c, :])
            else:
                nc.sync.dma_start(out=rows, in_=both[:])

        to_quantise = []
        for step in range(STEPS):
            for group, codes, scales in to_quantise:
                nc.vector.quantize_mx(out=codes.bitcast(FP8X4), scales=scales, in_=group)
            to_quantise = []
            outputs = unit_of(step, AT_OUTPUTS)
            next_outputs = unit_of(step + 1, AT_OUTPUTS)
            if next_outputs:
                output_weights(*next_outputs)

            e1_unit = unit_of(step, AT_E1)
            e2_unit = unit_of(step, AT_E2)
            rows_unit = unit_of(step, AT_ROWS)
            scores_unit = unit_of(step, AT_SCORES)
            inputs_unit = unit_of(step, AT_INPUTS)
            project_unit = unit_of(step, AT_PROJECT)
            if e1_unit:
                e1_rows = exp_columns(*e1_unit)

            if inputs_unit:
                to_quantise.extend(start_input(*inputs_unit))
            if step == AT_SCORES:
                transpose_mask()
            score_work = []
            if scores_unit:
                b, quarter = scores_unit
                score_work = [(b, 2 * (quarter % 2) + n, quarter // 2) for n in range(2)]
            input_work = [(inputs_unit[0], inputs_unit[1], n) for n in PIECE_ORDER if inputs_unit]
            if step == 0:
                input_work = [(0, 0, 0), (0, 0, 1), (0, 0, 2, slice(0, 1)), (0, 0, 2, slice(1, 2))]
            for n in range(max(PIECES, len(input_work))):
                if step == AT_SCORES and n < len(input_work):
                    transpose_input(*input_work[n])
                if n < len(score_work):
                    score_bank(*score_work[n])
                if step != AT_SCORES and n < len(input_work):
                    transpose_input(*input_work[n])
            if scores_unit and scores_unit[1] >= 2:
                for n in range(2):
                    column_shift(scores_unit[0], 2 * (scores_unit[1] - 2) + n)
            if inputs_unit and step + LOAD_AHEAD < UNITS:
                load(step + LOAD_AHEAD)

            banks = score_rows(*rows_unit) if rows_unit else []
            if step == AT_PROJECT - 1:
                to_quantise.append(transpose_wv())
            group = None
            if e1_unit or e2_unit:
                group, call = start_exponentials(e1_unit, e2_unit)
                to_quantise.append(call)
            late = step >= UNITS + AT_SCORES
            if late:
                if e2_unit:
                    transpose_exp(e2_rows[e2_unit], group[:, 1 if e1_unit else 0, :])
                if outputs:
                    x1_mid_rows(*outputs)
                    x2_out_rows(*outputs, 1)
                if rows_unit:
                    exp_rows(rows_unit[0], rows_unit[1], banks)
                if e1_unit:
                    transpose_exp(e1_rows, group[:, 0, :])
            else:
                if e1_unit:
                    transpose_exp(e1_rows, group[:, 0, :])
                if e2_unit:
                    transpose_exp(e2_rows[e2_unit], group[:, 1 if e1_unit else 0, :])
                if rows_unit:
                    exp_rows(rows_unit[0], rows_unit[1], banks)

            if project_unit:
                to_quantise.extend(project(*project_unit))
            if outputs and not late:
                x1_mid_rows(*outputs)
                x2_out_rows(*outputs, 0)
